import numpy as np
import ml_dtypes


def mxq(x, axis, fmt="e4m3"):
    dtype, down = {"e4m3": (ml_dtypes.float8_e4m3fn, 7), "e5m2": (ml_dtypes.float8_e5m2, 14)}[fmt]
    v = np.moveaxis(np.asarray(x, np.float32).astype(ml_dtypes.bfloat16).astype(np.float64), axis, -1)
    blocks = v.reshape(v.shape[:-1] + (-1, 32))
    amax = np.abs(blocks).max(-1, keepdims=True)
    byte = np.maximum(np.where(amax > 0, np.frexp(amax)[1] - 1 + 127, 0) - down, 1)
    scale = np.exp2(byte - 127.0)
    codes = (blocks / scale).astype(np.float32).astype(dtype).astype(np.float64)
    return np.moveaxis((codes * scale).reshape(v.shape), -1, axis)


WIDE = False


def mx_kscale(k):
    if not WIDE:
        return np.ones(k)
    levels = np.array([10, -10, 5, -5, 0])
    a = np.random.permutation(np.resize(levels, k // 512 * 4)).reshape(k // 512, 4)
    idx = np.arange(k)
    return np.exp2(a[idx // 512, idx % 128 // 32])


BF16 = ml_dtypes.bfloat16


def bf(x):
    return np.asarray(x, np.float32).astype(BF16)


def f64(x):
    return np.asarray(x).astype(np.float64)


E2M1 = np.array([0.0, 0.5, 1.0, 1.5, 2.0, 3.0, 4.0, 6.0, -0.0, -0.5, -1.0, -1.5, -2.0, -3.0, -4.0, -6.0])


def pack_weight(w, fmt):
    k, n = w.shape
    w = f64(bf(w)).reshape(k // 32, 32, n)
    amax = np.abs(w).max(1)
    if fmt == "e4m3":
        byte = np.frexp(amax)[1] - 1 + 127 - 7
    else:
        mant, ex = np.frexp(amax / 6.0)
        byte = np.where(mant > 0.5, ex, ex - 1) + 127
    byte = np.clip(np.where(amax > 0, byte, 1), 1, 254)
    scaled = (w * np.exp2(127.0 - byte)[:, None, :]).reshape(k, n).astype(np.float32)
    by_word = np.ascontiguousarray(scaled.reshape(k // 512, 128, 4, n).transpose(0, 1, 3, 2))
    if fmt == "e4m3":
        words = by_word.astype(ml_dtypes.float8_e4m3fn).view(np.uint8)
    else:
        c = by_word.astype(ml_dtypes.float4_e2m1fn).view(np.uint8) & 0xF
        words = c[..., 0::2] | (c[..., 1::2] << 4)
    return np.ascontiguousarray(words), np.ascontiguousarray(byte.astype(np.uint8).reshape(k // 512, 16, n))


def unpack_weight(words, scales, fmt):
    g, p, n, _ = words.shape
    if fmt == "e4m3":
        vals = np.ascontiguousarray(words).view(ml_dtypes.float8_e4m3fn).astype(np.float64)
    else:
        nib = np.empty((g, p, n, 4), np.uint8)
        nib[..., 0::2] = words & 0xF
        nib[..., 1::2] = words >> 4
        vals = E2M1[nib]
    vals = vals * np.repeat(np.exp2(scales.astype(np.float64) - 127.0), 8, axis=1)[..., None]
    return vals.transpose(0, 1, 3, 2).reshape(g * 512, n)

def pack4(w):
    words, scales = pack_weight(w, "e2m1")
    return words.reshape(words.shape[0], 128, -1), scales


def unpack4(words, scales):
    return unpack_weight(words.reshape(words.shape[0], 128, -1, 2), scales, "e2m1")


B, N, C, H, REG, QKV, LAYERS, PAIR = 1, 4096, 512, 4, 5, 3, 12, 2
D = C // H


def setup_inputs():
    s = mx_kscale(C)
    w = np.random.standard_normal((C, QKV * C)) * 1.5 / np.sqrt(C)
    m = np.random.standard_normal(C)
    al = np.random.standard_normal((B, N, 1))
    x = np.random.standard_normal((B, N, C)) + al * m
    gain = np.exp2(np.random.uniform(-1.0, 1.0, (H, 1)))
    g = ((m[:, None] * w[:, :C]).sum(0).reshape(H, D) + np.random.standard_normal((H, D))) * gain
    words, scales = pack4(w / s[:, None])
    return {"x": bf(x * s), "W_qkv_words": words, "W_qkv_scales": scales, "q_g": bf(g)}


def reference(x, W_qkv_words, W_qkv_scales, q_g):
    qkv = (mxq(f64(x), 2, "e4m3") @ unpack4(W_qkv_words, W_qkv_scales)).reshape(B, N, QKV, H, D)
    q, k, v = qkv[:, :, 0], qkv[:, :, 1], qkv[:, :, 2]
    q_pure = q[:, REG:]
    q_n = q_pure / np.sqrt((q_pure ** 2).sum(-1, keepdims=True))
    g = f64(q_g)
    qg_n = g / np.sqrt((g ** 2).sum(-1, keepdims=True))
    sim = (qg_n[None, None] * q_n).sum(-1).mean(-1)
    return q, k, v, sim

@@ -1,0 +1,227 @@
+from contextlib import ExitStack
+
+import concourse.mybir as mybir
+from concourse.masks import make_identity
+
+F32 = mybir.dt.float32
+BF16 = mybir.dt.bfloat16
+I32 = mybir.dt.int32
+U32 = mybir.dt.uint32
+U8 = mybir.dt.uint8
+FP8X4 = mybir.dt.float8_e4m3fn_x4
+FP4X4 = mybir.dt.float4_e2m1fn_x4
+ACT = mybir.ActivationFunctionType
+ALU = mybir.AluOpType
+
+P = 128
+TOKENS = 4096
+K = 512
+HEADS = 4
+HEAD_DIM = 128
+WIDTH = HEADS * HEAD_DIM
+REGISTERS = 5
+TILES = TOKENS // P
+PAIR = 2
+PAIRS = TILES // PAIR
+WORDS = K // 2
+PRODUCTS_LAG = 2
+FIRST_ROW_RUNS = 3
+FIRST_ROW_RUN = (TILES - REGISTERS) // FIRST_ROW_RUNS
+
+FLOPS = 2 * TOKENS * K * 3 * WIDTH
+
+
+def tile_memeffattention_pa_t_kernel(tc, x, W_qkv_words, W_qkv_scales, q_g, out_0, out_1, out_2, out_3):
+    nc = tc.nc
+    x_tiles = x[0].rearrange("(p t) c -> p t c", t=TILES)
+    qkv_tiles = [o[0].rearrange("(p t) h d -> p t (h d)", t=TILES) for o in (out_0, out_1, out_2)]
+
+    with ExitStack() as ctx:
+        const = ctx.enter_context(tc.tile_pool(name="const", bufs=1))
+        x_pool = ctx.enter_context(tc.tile_pool(name="x_pool", bufs=PAIRS))
+        prep = ctx.enter_context(tc.tile_pool(name="prep", bufs=4))
+        results = ctx.enter_context(tc.tile_pool(name="results", bufs=6))
+        scrap = ctx.enter_context(tc.tile_pool(name="scrap", bufs=2))
+        products_pool = ctx.enter_context(tc.tile_pool(name="products_pool", bufs=PRODUCTS_LAG + 3))
+        psum_xt = ctx.enter_context(tc.psum_pool(name="psum_xt", bufs=2))
+        psum_acc = ctx.enter_context(tc.psum_pool(name="psum_acc", bufs=2))
+        ctx.enter_context(tc.manual_schedule())
+
+        g_rows = const.tile([P, WIDTH], BF16)
+        nc.vector.memset(g_rows[:], 0.0)
+        nc.scalar.dma_start(out=g_rows[0:1, :], in_=q_g.rearrange("(o h) d -> o (h d)", o=1))
+        w_scales = const.tile([P, 3 * WIDTH], U8, align_bytes=64)
+        nc.vector.memset(w_scales[:].bitcast(I32), 0)
+        ones = const.tile([P, P], BF16)
+        nc.vector.memset(ones[:], 1.0)
+        identity = const.tile([P, P], F32)
+        make_identity(nc, identity[:])
+
+        one = const.tile([P, 1], F32)
+        nc.vector.memset(one[:], 1.0)
+        nc.scalar.activation(out=one[:], in_=one[:], func=ACT.Sqrt)
+
+        def load_x(j):
+            x_sb = x_pool.tile([P, PAIR, K], BF16)
+            nc.sync.dma_start(out=x_sb[:], in_=x_tiles[:, j * PAIR : (j + 1) * PAIR, :])
+            return x_sb
+
+        x_loaded = [load_x(0)]
+        w_words = const.tile([P, 2 * 3 * WIDTH], U8, align_bytes=64)
+        nc.sync.dma_start(out=w_words[:].bitcast(I32), in_=W_qkv_words[0].bitcast(I32))
+        for quadrant in range(4):
+            nc.sync.dma_start(
+                out=w_scales[32 * quadrant : 32 * quadrant + 4, :].bitcast(I32),
+                in_=W_qkv_scales[0, 4 * quadrant : 4 * quadrant + 4, :].bitcast(I32),
+            )
+        x_loaded.extend([load_x(j) for j in range(1, PAIRS)])
+
+        g_bank = psum_acc.tile([P, WIDTH], F32, tag="acc0")
+        nc.tensor.matmul(out=g_bank[:], lhsT=ones[:], rhs=g_rows[:], start=True, stop=True)
+        g_all = const.tile([P, WIDTH], F32)
+        nc.scalar.copy(out=g_all[:], in_=g_bank[:])
+
+        def sums_of_squares(rows, totals):
+            for h in range(HEADS):
+                squares = scrap.tile([P, HEAD_DIM], F32)
+                nc.scalar.activation(
+                    out=squares[:],
+                    in_=rows[:, h * HEAD_DIM : (h + 1) * HEAD_DIM],
+                    func=ACT.Square,
+                    accum_out=totals[:, h : h + 1],
+                )
+
+        q_sumsq = const.tile([P, TILES * HEADS], F32)
+        q_dot_g = const.tile([P, TILES * HEADS], F32)
+
+        grouped_pairs = []
+        quantised_pairs = []
+        products_of = []
+
+        def regroup_next_pair():
+            j = len(grouped_pairs)
+            if j == PAIRS:
+                return
+            xt = psum_xt.tile([P, PAIR, 2, P], F32)
+            for i in range(PAIR):
+                words = x_loaded[j][:, i, :].bitcast(F32)
+                for u in range(2):
+                    nc.tensor.transpose(xt[:, i, u, :], words[:, u:WORDS:2], identity[:])
+            grouped = prep.tile([P, PAIR * P * 4], BF16, align_bytes=64)
+            nc.scalar.copy(
+                out=grouped[:].bitcast(F32).rearrange("p (i r u) -> p i r u", i=PAIR, u=2),
+                in_=xt[:].rearrange("p i u r -> p i r u"),
+            )
+            grouped_pairs.append(grouped)
+
+        def quantise_next_pair():
+            j = len(quantised_pairs)
+            if j == PAIRS:
+                return
+            codes = prep.tile([P, PAIR * P], U32, align_bytes=64)
+            scales = prep.tile([P, PAIR * P], U8, align_bytes=64)
+            nc.vector.quantize_mx(out=codes[:].bitcast(FP8X4), scales=scales[:], in_=grouped_pairs[j][:])
+            quantised_pairs.append((codes, scales))
+
+        def take(copy, t, o, result):
+            j, i = divmod(t, PAIR)
+            codes, scales = quantised_pairs[j]
+            tokens = slice(i * P, (i + 1) * P)
+            acc = psum_acc.tile([P, WIDTH], F32, name="acc%d" % o, tag="acc%d" % o)
+            nc.tensor.matmul_mx(
+                out=acc[:],
+                lhsT=codes[:, tokens].bitcast(FP8X4),
+                lhsT_scale=scales[:, tokens],
+                rhs=w_words[:, 2 * o * WIDTH : 2 * (o + 1) * WIDTH].bitcast(FP4X4),
+                rhs_scale=w_scales[:, o * WIDTH : (o + 1) * WIDTH],
+                start=True,
+                stop=True,
+            )
+            copy(out=result[:, i, :], in_=acc[:])
+            if i == PAIR - 1:
+                nc.sync.dma_start(out=qkv_tiles[o][:, PAIR * j : PAIR * (j + 1), :], in_=result[:])
+
+        def take_q(t, q_sb):
+            take(nc.vector.tensor_copy, t, 0, q_sb)
+            products = products_pool.tile([P, HEADS, HEAD_DIM], F32)
+            nc.gpsimd.tensor_mul(
+                out=products[:].rearrange("p h d -> p (h d)"), in0=q_sb[:, t % PAIR, :], in1=g_all[:]
+            )
+            products_of.append(products)
+
+        def add_products(t):
+            nc.vector.tensor_reduce(
+                out=q_dot_g[:, t * HEADS : (t + 1) * HEADS],
+                in_=products_of[t][:],
+                axis=mybir.AxisListType.X,
+                op=ALU.add,
+            )
+
+        def finish_tile(t, q_sb, v_sb):
+            take(nc.scalar.copy, t, 2, v_sb)
+            sums_of_squares(q_sb[:, t % PAIR, :], q_sumsq[:, t * HEADS : (t + 1) * HEADS])
+            if t >= PRODUCTS_LAG:
+                add_products(t - PRODUCTS_LAG)
+
+        regroup_next_pair()
+        quantise_next_pair()
+        g_sumsq = const.tile([P, HEADS], F32)
+        sums_of_squares(g_all, g_sumsq)
+        g_norm_x4 = const.tile([P, HEADS], F32)
+        nc.scalar.activation(out=g_norm_x4[:], in_=g_sumsq[:], func=ACT.Sqrt, scale=16.0)
+        regroup_next_pair()
+        regroup_next_pair()
+        for a in range(0, TILES, 2 * PAIR):
+            b, c, d = a + 1, a + 2, a + 3
+            q_ab = results.tile([P, PAIR, WIDTH], F32, tag="q")
+            k_ab = results.tile([P, PAIR, WIDTH], F32, tag="k")
+            v_ab = results.tile([P, PAIR, WIDTH], F32, tag="v")
+            take_q(a, q_ab)
+            take(nc.vector.tensor_copy, a, 1, k_ab)
+            finish_tile(a, q_ab, v_ab)
+            take(nc.vector.tensor_copy, b, 1, k_ab)
+            quantise_next_pair()
+            quantise_next_pair()
+            take_q(b, q_ab)
+            finish_tile(b, q_ab, v_ab)
+            regroup_next_pair()
+
+            q_cd = results.tile([P, PAIR, WIDTH], F32, tag="q")
+            k_cd = results.tile([P, PAIR, WIDTH], F32, tag="k")
+            v_cd = results.tile([P, PAIR, WIDTH], F32, tag="v")
+            take_q(c, q_cd)
+            take(nc.vector.tensor_copy, c, 1, k_cd)
+            finish_tile(c, q_cd, v_cd)
+            take_q(d, q_cd)
+            take(nc.scalar.copy, d, 1, k_cd)
+            finish_tile(d, q_cd, v_cd)
+            regroup_next_pair()
+
+        denominator = const.tile([P, TILES, HEADS], F32)
+        nc.scalar.activation(out=denominator[:].rearrange("p t h -> p (t h)"), in_=q_sumsq[:], func=ACT.Sqrt)
+        nc.vector.tensor_mul(
+            out=denominator[:],
+            in0=denominator[:],
+            in1=g_norm_x4[:].unsqueeze(1).to_broadcast([P, TILES, HEADS]),
+        )
+        nc.vector.reciprocal(out=denominator[:], in_=denominator[:])
+        for t in range(TILES - PRODUCTS_LAG, TILES):
+            add_products(t)
+        cosines = const.tile([P, TILES, HEADS], F32)
+        nc.vector.tensor_mul(
+            out=cosines[:], in0=q_dot_g[:].rearrange("p (t h) -> p t h", h=HEADS), in1=denominator[:]
+        )
+        sim = const.tile([P, TILES], F32)
+        nc.vector.tensor_reduce(out=sim[:], in_=cosines[:], axis=mybir.AxisListType.X, op=ALU.add)
+        whole_rows = out_3[0, TILES - REGISTERS : TOKENS - REGISTERS].rearrange("(p t) -> p t", t=TILES)
+        nc.sync.dma_start(out=whole_rows[0 : P // 2, :], in_=sim[1 : 1 + P // 2, :])
+        nc.sync.dma_start(out=whole_rows[P // 2 : P - 1, :], in_=sim[1 + P // 2 : P, :])
+        first_row = const.tile([P, FIRST_ROW_RUNS, 2 * FIRST_ROW_RUN], F32)
+        nc.vector.tensor_copy(
+            out=first_row[0:1, :, 0:FIRST_ROW_RUN],
+            in_=sim[0:1, REGISTERS:TILES].rearrange("o (r c) -> o r c", c=FIRST_ROW_RUN),
+        )
+        nc.sync.dma_start(
+            out=out_3[0:1, 0 : TILES - REGISTERS].rearrange("o (r c) -> o r c", c=FIRST_ROW_RUN),
+            in_=first_row[0:1, :, 0:FIRST_ROW_RUN],
+        )

@@ -24,6 +24,9 @@ TILES = TOKENS // P
 PAIR = 2
 PAIRS = TILES // PAIR
 WORDS = K // 2
+ROUND = 2 * PAIR
+ROUNDS = TILES // ROUND
+LEAD = 1
 PRODUCTS_LAG = 2
 FIRST_ROW_RUNS = 3
 FIRST_ROW_RUN = (TILES - REGISTERS) // FIRST_ROW_RUNS
@@ -40,6 +43,7 @@ def tile_memeffattention_pa_t_kernel(tc, x, W_qkv_words, W_qkv_scales, q_g, out_
         const = ctx.enter_context(tc.tile_pool(name="const", bufs=1))
         x_pool = ctx.enter_context(tc.tile_pool(name="x_pool", bufs=PAIRS))
         prep = ctx.enter_context(tc.tile_pool(name="prep", bufs=4))
+        quantised = ctx.enter_context(tc.tile_pool(name="quantised", bufs=2 * LEAD + 4))
         results = ctx.enter_context(tc.tile_pool(name="results", bufs=6))
         scrap = ctx.enter_context(tc.tile_pool(name="scrap", bufs=2))
         products_pool = ctx.enter_context(tc.tile_pool(name="products_pool", bufs=PRODUCTS_LAG + 3))
@@ -118,8 +122,8 @@ def tile_memeffattention_pa_t_kernel(tc, x, W_qkv_words, W_qkv_scales, q_g, out_
             j = len(quantised_pairs)
             if j == PAIRS:
                 return
-            codes = prep.tile([P, PAIR * P], U32, align_bytes=64)
-            scales = prep.tile([P, PAIR * P], U8, align_bytes=64)
+            codes = quantised.tile([P, PAIR * P], U32, align_bytes=64)
+            scales = quantised.tile([P, PAIR * P], U8, align_bytes=64)
             nc.vector.quantize_mx(out=codes[:].bitcast(FP8X4), scales=scales[:], in_=grouped_pairs[j][:])
             quantised_pairs.append((codes, scales))
 
@@ -157,11 +161,36 @@ def tile_memeffattention_pa_t_kernel(tc, x, W_qkv_words, W_qkv_scales, q_g, out_
                 op=ALU.add,
             )
 
-        def finish_tile(t, q_sb, v_sb):
-            take(nc.scalar.copy, t, 2, v_sb)
+        def after_q(t, q_sb):
             sums_of_squares(q_sb[:, t % PAIR, :], q_sumsq[:, t * HEADS : (t + 1) * HEADS])
             if t >= PRODUCTS_LAG:
                 add_products(t - PRODUCTS_LAG)
+
+        def similarity():
+            nc.vector.tensor_mul(
+                out=denominator[:],
+                in0=denominator[:],
+                in1=g_norm_x4[:].unsqueeze(1).to_broadcast([P, TILES, HEADS]),
+            )
+            nc.vector.reciprocal(out=denominator[:], in_=denominator[:])
+            cosines = const.tile([P, TILES, HEADS], F32)
+            nc.vector.tensor_mul(
+                out=cosines[:], in0=q_dot_g[:].rearrange("p (t h) -> p t h", h=HEADS), in1=denominator[:]
+            )
+            sim = const.tile([P, TILES], F32)
+            nc.vector.tensor_reduce(out=sim[:], in_=cosines[:], axis=mybir.AxisListType.X, op=ALU.add)
+            first_row = const.tile([P, FIRST_ROW_RUNS, 2 * FIRST_ROW_RUN], F32)
+            nc.vector.tensor_copy(
+                out=first_row[0:1, :, 0:FIRST_ROW_RUN],
+                in_=sim[0:1, REGISTERS:TILES].rearrange("o (r c) -> o r c", c=FIRST_ROW_RUN),
+            )
+            whole_rows = out_3[0, TILES - REGISTERS : TOKENS - REGISTERS].rearrange("(p t) -> p t", t=TILES)
+            nc.sync.dma_start(out=whole_rows[0 : P // 2, :], in_=sim[1 : 1 + P // 2, :])
+            nc.sync.dma_start(out=whole_rows[P // 2 : P - 1, :], in_=sim[1 + P // 2 : P, :])
+            nc.sync.dma_start(
+                out=out_3[0:1, 0 : TILES - REGISTERS].rearrange("o (r c) -> o r c", c=FIRST_ROW_RUN),
+                in_=first_row[0:1, :, 0:FIRST_ROW_RUN],
+            )
 
         regroup_next_pair()
         quantise_next_pair()
@@ -171,57 +200,57 @@ def tile_memeffattention_pa_t_kernel(tc, x, W_qkv_words, W_qkv_scales, q_g, out_
         nc.scalar.activation(out=g_norm_x4[:], in_=g_sumsq[:], func=ACT.Sqrt, scale=16.0)
         regroup_next_pair()
         regroup_next_pair()
-        for a in range(0, TILES, 2 * PAIR):
-            b, c, d = a + 1, a + 2, a + 3
-            q_ab = results.tile([P, PAIR, WIDTH], F32, tag="q")
-            k_ab = results.tile([P, PAIR, WIDTH], F32, tag="k")
-            v_ab = results.tile([P, PAIR, WIDTH], F32, tag="v")
-            take_q(a, q_ab)
-            take(nc.vector.tensor_copy, a, 1, k_ab)
-            finish_tile(a, q_ab, v_ab)
-            take(nc.vector.tensor_copy, b, 1, k_ab)
-            quantise_next_pair()
-            quantise_next_pair()
-            take_q(b, q_ab)
-            finish_tile(b, q_ab, v_ab)
-            regroup_next_pair()
-
-            q_cd = results.tile([P, PAIR, WIDTH], F32, tag="q")
-            k_cd = results.tile([P, PAIR, WIDTH], F32, tag="k")
-            v_cd = results.tile([P, PAIR, WIDTH], F32, tag="v")
-            take_q(c, q_cd)
-            take(nc.vector.tensor_copy, c, 1, k_cd)
-            finish_tile(c, q_cd, v_cd)
-            take_q(d, q_cd)
-            take(nc.scalar.copy, d, 1, k_cd)
-            finish_tile(d, q_cd, v_cd)
-            regroup_next_pair()
-
         denominator = const.tile([P, TILES, HEADS], F32)
-        nc.scalar.activation(out=denominator[:].rearrange("p t h -> p (t h)"), in_=q_sumsq[:], func=ACT.Sqrt)
-        nc.vector.tensor_mul(
-            out=denominator[:],
-            in0=denominator[:],
-            in1=g_norm_x4[:].unsqueeze(1).to_broadcast([P, TILES, HEADS]),
-        )
-        nc.vector.reciprocal(out=denominator[:], in_=denominator[:])
-        for t in range(TILES - PRODUCTS_LAG, TILES):
-            add_products(t)
-        cosines = const.tile([P, TILES, HEADS], F32)
-        nc.vector.tensor_mul(
-            out=cosines[:], in0=q_dot_g[:].rearrange("p (t h) -> p t h", h=HEADS), in1=denominator[:]
-        )
-        sim = const.tile([P, TILES], F32)
-        nc.vector.tensor_reduce(out=sim[:], in_=cosines[:], axis=mybir.AxisListType.X, op=ALU.add)
-        whole_rows = out_3[0, TILES - REGISTERS : TOKENS - REGISTERS].rearrange("(p t) -> p t", t=TILES)
-        nc.sync.dma_start(out=whole_rows[0 : P // 2, :], in_=sim[1 : 1 + P // 2, :])
-        nc.sync.dma_start(out=whole_rows[P // 2 : P - 1, :], in_=sim[1 + P // 2 : P, :])
-        first_row = const.tile([P, FIRST_ROW_RUNS, 2 * FIRST_ROW_RUN], F32)
-        nc.vector.tensor_copy(
-            out=first_row[0:1, :, 0:FIRST_ROW_RUN],
-            in_=sim[0:1, REGISTERS:TILES].rearrange("o (r c) -> o r c", c=FIRST_ROW_RUN),
-        )
-        nc.sync.dma_start(
-            out=out_3[0:1, 0 : TILES - REGISTERS].rearrange("o (r c) -> o r c", c=FIRST_ROW_RUN),
-            in_=first_row[0:1, :, 0:FIRST_ROW_RUN],
-        )
+        for r in range(ROUNDS + LEAD):
+            with_q = r < ROUNDS
+            with_kv = r >= LEAD
+            qa = ROUND * r
+            ka = ROUND * (r - LEAD)
+            if r == ROUNDS:
+                nc.scalar.activation(
+                    out=denominator[:].rearrange("p t h -> p (t h)"), in_=q_sumsq[:], func=ACT.Sqrt
+                )
+                add_products(TILES - 2)
+            if with_q:
+                q_ab = results.tile([P, PAIR, WIDTH], F32, tag="q")
+                take_q(qa, q_ab)
+            if with_kv:
+                k_ab = results.tile([P, PAIR, WIDTH], F32, tag="k")
+                v_ab = results.tile([P, PAIR, WIDTH], F32, tag="v")
+                take(nc.vector.tensor_copy, ka, 1, k_ab)
+                take(nc.scalar.copy, ka, 2, v_ab)
+            if with_q:
+                after_q(qa, q_ab)
+            if r == ROUNDS:
+                add_products(TILES - 1)
+            if with_kv:
+                take(nc.vector.tensor_copy if with_q else nc.scalar.copy, ka + 1, 1, k_ab)
+            quantise_next_pair()
+            quantise_next_pair()
+            if with_q:
+                take_q(qa + 1, q_ab)
+            if with_kv:
+                take(nc.scalar.copy, ka + 1, 2, v_ab)
+            if with_q:
+                after_q(qa + 1, q_ab)
+            regroup_next_pair()
+            if r == ROUNDS:
+                similarity()
+
+            if with_q:
+                q_cd = results.tile([P, PAIR, WIDTH], F32, tag="q")
+                take_q(qa + 2, q_cd)
+            if with_kv:
+                k_cd = results.tile([P, PAIR, WIDTH], F32, tag="k")
+                v_cd = results.tile([P, PAIR, WIDTH], F32, tag="v")
+                take(nc.vector.tensor_copy, ka + 2, 1, k_cd)
+                take(nc.scalar.copy, ka + 2, 2, v_cd)
+            if with_q:
+                after_q(qa + 2, q_cd)
+                take_q(qa + 3, q_cd)
+            if with_kv:
+                take(nc.scalar.copy if with_q else nc.vector.tensor_copy, ka + 3, 1, k_cd)
+                take(nc.scalar.copy, ka + 3, 2, v_cd)
+            if with_q:
+                after_q(qa + 3, q_cd)
+            regroup_next_pair()

@@ -27,6 +27,7 @@ WORDS = K // 2
 ROUND = 2 * PAIR
 ROUNDS = TILES // ROUND
 LEAD = 1
+SQUARES_LAG = 1
 PRODUCTS_LAG = 2
 FIRST_ROW_RUNS = 3
 FIRST_ROW_RUN = (TILES - REGISTERS) // FIRST_ROW_RUNS
@@ -80,11 +81,6 @@ def tile_memeffattention_pa_t_kernel(tc, x, W_qkv_words, W_qkv_scales, q_g, out_
             )
         x_loaded.extend([load_x(j) for j in range(1, PAIRS)])
 
-        g_bank = psum_acc.tile([P, WIDTH], F32, tag="acc0")
-        nc.tensor.matmul(out=g_bank[:], lhsT=ones[:], rhs=g_rows[:], start=True, stop=True)
-        g_all = const.tile([P, WIDTH], F32)
-        nc.scalar.copy(out=g_all[:], in_=g_bank[:])
-
         def sums_of_squares(rows, totals):
             for h in range(HEADS):
                 squares = scrap.tile([P, HEAD_DIM], F32)
@@ -102,7 +98,7 @@ def tile_memeffattention_pa_t_kernel(tc, x, W_qkv_words, W_qkv_scales, q_g, out_
         quantised_pairs = []
         products_of = []
 
-        def regroup_next_pair():
+        def regroup_next_pair(copy=nc.scalar.copy):
             j = len(grouped_pairs)
             if j == PAIRS:
                 return
@@ -112,7 +108,7 @@ def tile_memeffattention_pa_t_kernel(tc, x, W_qkv_words, W_qkv_scales, q_g, out_
                 for u in range(2):
                     nc.tensor.transpose(xt[:, i, u, :], words[:, u:WORDS:2], identity[:])
             grouped = prep.tile([P, PAIR * P * 4], BF16, align_bytes=64)
-            nc.scalar.copy(
+            copy(
                 out=grouped[:].bitcast(F32).rearrange("p (i r u) -> p i r u", i=PAIR, u=2),
                 in_=xt[:].rearrange("p i u r -> p i r u"),
             )
@@ -161,8 +157,15 @@ def tile_memeffattention_pa_t_kernel(tc, x, W_qkv_words, W_qkv_scales, q_g, out_
                 op=ALU.add,
             )
 
+        q_rows_of = []
+
+        def square_q(t):
+            sums_of_squares(q_rows_of[t], q_sumsq[:, t * HEADS : (t + 1) * HEADS])
+
         def after_q(t, q_sb):
-            sums_of_squares(q_sb[:, t % PAIR, :], q_sumsq[:, t * HEADS : (t + 1) * HEADS])
+            q_rows_of.append(q_sb[:, t % PAIR, :])
+            if t >= SQUARES_LAG:
+                square_q(t - SQUARES_LAG)
             if t >= PRODUCTS_LAG:
                 add_products(t - PRODUCTS_LAG)
 
@@ -192,14 +195,17 @@ def tile_memeffattention_pa_t_kernel(tc, x, W_qkv_words, W_qkv_scales, q_g, out_
                 in_=first_row[0:1, :, 0:FIRST_ROW_RUN],
             )
 
-        regroup_next_pair()
+        regroup_next_pair(nc.vector.tensor_copy)
         quantise_next_pair()
+        g_bank = psum_acc.tile([P, WIDTH], F32, tag="acc2")
+        nc.tensor.matmul(out=g_bank[:], lhsT=ones[:], rhs=g_rows[:], start=True, stop=True)
+        g_all = const.tile([P, WIDTH], F32)
+        nc.scalar.copy(out=g_all[:], in_=g_bank[:])
         g_sumsq = const.tile([P, HEADS], F32)
-        sums_of_squares(g_all, g_sumsq)
         g_norm_x4 = const.tile([P, HEADS], F32)
+        sums_of_squares(g_all, g_sumsq)
         nc.scalar.activation(out=g_norm_x4[:], in_=g_sumsq[:], func=ACT.Sqrt, scale=16.0)
-        regroup_next_pair()
-        regroup_next_pair()
+        regroup_next_pair(nc.vector.tensor_copy)
         denominator = const.tile([P, TILES, HEADS], F32)
         for r in range(ROUNDS + LEAD):
             with_q = r < ROUNDS
@@ -207,6 +213,8 @@ def tile_memeffattention_pa_t_kernel(tc, x, W_qkv_words, W_qkv_scales, q_g, out_
             qa = ROUND * r
             ka = ROUND * (r - LEAD)
             if r == ROUNDS:
+                for t in range(TILES - SQUARES_LAG, TILES):
+                    square_q(t)
                 nc.scalar.activation(
                     out=denominator[:].rearrange("p t h -> p (t h)"), in_=q_sumsq[:], func=ACT.Sqrt
                 )
@@ -214,6 +222,8 @@ def tile_memeffattention_pa_t_kernel(tc, x, W_qkv_words, W_qkv_scales, q_g, out_
             if with_q:
                 q_ab = results.tile([P, PAIR, WIDTH], F32, tag="q")
                 take_q(qa, q_ab)
+            if r == 0:
+                regroup_next_pair()
             if with_kv:
                 k_ab = results.tile([P, PAIR, WIDTH], F32, tag="k")
                 v_ab = results.tile([P, PAIR, WIDTH], F32, tag="v")
@@ -226,9 +236,12 @@ def tile_memeffattention_pa_t_kernel(tc, x, W_qkv_words, W_qkv_scales, q_g, out_
             if with_kv:
                 take(nc.vector.tensor_copy if with_q else nc.scalar.copy, ka + 1, 1, k_ab)
             quantise_next_pair()
-            quantise_next_pair()
+            if r > 0:
+                quantise_next_pair()
             if with_q:
                 take_q(qa + 1, q_ab)
+            if r == 0:
+                quantise_next_pair()
             if with_kv:
                 take(nc.scalar.copy, ka + 1, 2, v_ab)
             if with_q:

@@ -207,11 +207,11 @@ def tile_memeffattention_pa_t_kernel(tc, x, W_qkv_words, W_qkv_scales, q_g, out_
         nc.scalar.activation(out=g_norm_x4[:], in_=g_sumsq[:], func=ACT.Sqrt, scale=16.0)
         regroup_next_pair(nc.vector.tensor_copy)
         denominator = const.tile([P, TILES, HEADS], F32)
-        for r in range(ROUNDS + LEAD):
+        for r in range(ROUNDS + 1):
             with_q = r < ROUNDS
-            with_kv = r >= LEAD
+            with_kv = r > 0
             qa = ROUND * r
-            ka = ROUND * (r - LEAD)
+            ka = qa - PAIR
             if r == ROUNDS:
                 for t in range(TILES - SQUARES_LAG, TILES):
                     square_q(t)
@@ -252,18 +252,14 @@ def tile_memeffattention_pa_t_kernel(tc, x, W_qkv_words, W_qkv_scales, q_g, out_
 
             if with_q:
                 q_cd = results.tile([P, PAIR, WIDTH], F32, tag="q")
-                take_q(qa + 2, q_cd)
-            if with_kv:
                 k_cd = results.tile([P, PAIR, WIDTH], F32, tag="k")
                 v_cd = results.tile([P, PAIR, WIDTH], F32, tag="v")
+                take_q(qa + 2, q_cd)
                 take(nc.vector.tensor_copy, ka + 2, 1, k_cd)
                 take(nc.scalar.copy, ka + 2, 2, v_cd)
-            if with_q:
                 after_q(qa + 2, q_cd)
                 take_q(qa + 3, q_cd)
-            if with_kv:
-                take(nc.scalar.copy if with_q else nc.vector.tensor_copy, ka + 3, 1, k_cd)
+                take(nc.scalar.copy, ka + 3, 1, k_cd)
                 take(nc.scalar.copy, ka + 3, 2, v_cd)
-            if with_q:
                 after_q(qa + 3, q_cd)
-            regroup_next_pair()
+                regroup_next_pair()

@@ -27,6 +27,7 @@ WORDS = K // 2
 ROUND = 2 * PAIR
 ROUNDS = TILES // ROUND
 LEAD = 1
+WARM_UP = 3
 SQUARES_LAG = 1
 PRODUCTS_LAG = 2
 FIRST_ROW_RUNS = 3
@@ -52,6 +53,11 @@ def tile_memeffattention_pa_t_kernel(tc, x, W_qkv_words, W_qkv_scales, q_g, out_
         psum_acc = ctx.enter_context(tc.psum_pool(name="psum_acc", bufs=2))
         ctx.enter_context(tc.manual_schedule())
 
+        zeros = const.tile([P, WIDTH], BF16)
+        nc.gpsimd.memset(zeros[:], 0.0)
+        warm_bank = psum_acc.tile([P, WIDTH], F32, tag="acc1")
+        for i in range(WARM_UP):
+            nc.tensor.matmul(out=warm_bank[:], lhsT=zeros[:, 0:P], rhs=zeros[:], start=True, stop=True)
         g_rows = const.tile([P, WIDTH], BF16)
         nc.vector.memset(g_rows[:], 0.0)
         nc.scalar.dma_start(out=g_rows[0:1, :], in_=q_g.rearrange("(o h) d -> o (h d)", o=1))

@@ -24,12 +24,9 @@ TILES = TOKENS // P
 PAIR = 2
 PAIRS = TILES // PAIR
 WORDS = K // 2
-ROUND = 2 * PAIR
-ROUNDS = TILES // ROUND
-LEAD = 1
+STATS = 3
+RESULT_BUFS = 12
 WARM_UP = 3
-SQUARES_LAG = 1
-PRODUCTS_LAG = 2
 FIRST_ROW_RUNS = 3
 FIRST_ROW_RUN = (TILES - REGISTERS) // FIRST_ROW_RUNS
 
@@ -45,10 +42,10 @@ def tile_memeffattention_pa_t_kernel(tc, x, W_qkv_words, W_qkv_scales, q_g, out_
         const = ctx.enter_context(tc.tile_pool(name="const", bufs=1))
         x_pool = ctx.enter_context(tc.tile_pool(name="x_pool", bufs=PAIRS))
         prep = ctx.enter_context(tc.tile_pool(name="prep", bufs=4))
-        quantised = ctx.enter_context(tc.tile_pool(name="quantised", bufs=2 * LEAD + 4))
-        results = ctx.enter_context(tc.tile_pool(name="results", bufs=6))
+        quantised = ctx.enter_context(tc.tile_pool(name="quantised", bufs=6))
+        results = ctx.enter_context(tc.tile_pool(name="results", bufs=RESULT_BUFS))
         scrap = ctx.enter_context(tc.tile_pool(name="scrap", bufs=2))
-        products_pool = ctx.enter_context(tc.tile_pool(name="products_pool", bufs=PRODUCTS_LAG + 3))
+        products_pool = ctx.enter_context(tc.tile_pool(name="products_pool", bufs=3))
         psum_xt = ctx.enter_context(tc.psum_pool(name="psum_xt", bufs=2))
         psum_acc = ctx.enter_context(tc.psum_pool(name="psum_acc", bufs=2))
         ctx.enter_context(tc.manual_schedule())
@@ -87,25 +84,16 @@ def tile_memeffattention_pa_t_kernel(tc, x, W_qkv_words, W_qkv_scales, q_g, out_
             )
         x_loaded.extend([load_x(j) for j in range(1, PAIRS)])
 
-        def sums_of_squares(rows, totals):
-            for h in range(HEADS):
-                squares = scrap.tile([P, HEAD_DIM], F32)
-                nc.scalar.activation(
-                    out=squares[:],
-                    in_=rows[:, h * HEAD_DIM : (h + 1) * HEAD_DIM],
-                    func=ACT.Square,
-                    accum_out=totals[:, h : h + 1],
-                )
-
-        q_sumsq = const.tile([P, TILES * HEADS], F32)
+        q_stats = const.tile([P, TILES, HEADS, STATS], F32)
         q_dot_g = const.tile([P, TILES * HEADS], F32)
 
+        transposed_pairs = []
         grouped_pairs = []
         quantised_pairs = []
         products_of = []
 
-        def regroup_next_pair(copy=nc.scalar.copy):
-            j = len(grouped_pairs)
+        def transpose_next_pair():
+            j = len(transposed_pairs)
             if j == PAIRS:
                 return
             xt = psum_xt.tile([P, PAIR, 2, P], F32)
@@ -113,10 +101,16 @@ def tile_memeffattention_pa_t_kernel(tc, x, W_qkv_words, W_qkv_scales, q_g, out_
                 words = x_loaded[j][:, i, :].bitcast(F32)
                 for u in range(2):
                     nc.tensor.transpose(xt[:, i, u, :], words[:, u:WORDS:2], identity[:])
+            transposed_pairs.append(xt)
+
+        def regroup_next_pair(copy):
+            j = len(grouped_pairs)
+            if j == PAIRS:
+                return
             grouped = prep.tile([P, PAIR * P * 4], BF16, align_bytes=64)
             copy(
                 out=grouped[:].bitcast(F32).rearrange("p (i r u) -> p i r u", i=PAIR, u=2),
-                in_=xt[:].rearrange("p i u r -> p i r u"),
+                in_=transposed_pairs[j][:].rearrange("p i u r -> p i r u"),
             )
             grouped_pairs.append(grouped)
 
@@ -147,60 +141,27 @@ def tile_memeffattention_pa_t_kernel(tc, x, W_qkv_words, W_qkv_scales, q_g, out_
             if i == PAIR - 1:
                 nc.sync.dma_start(out=qkv_tiles[o][:, PAIR * j : PAIR * (j + 1), :], in_=result[:])
 
-        def take_q(t, q_sb):
-            take(nc.vector.tensor_copy, t, 0, q_sb)
-            products = products_pool.tile([P, HEADS, HEAD_DIM], F32)
+        def multiply_by_g(products, i, q_ab):
             nc.gpsimd.tensor_mul(
-                out=products[:].rearrange("p h d -> p (h d)"), in0=q_sb[:, t % PAIR, :], in1=g_all[:]
+                out=products[:, i, :, :].rearrange("p h d -> p (h d)"), in0=q_ab[:, i, :], in1=g_all[:]
             )
-            products_of.append(products)
 
-        def add_products(t):
+        def add_products(j):
             nc.vector.tensor_reduce(
-                out=q_dot_g[:, t * HEADS : (t + 1) * HEADS],
-                in_=products_of[t][:],
+                out=q_dot_g[:, j * PAIR * HEADS : (j + 1) * PAIR * HEADS],
+                in_=products_of[j][:].rearrange("p i h d -> p (i h) d"),
                 axis=mybir.AxisListType.X,
                 op=ALU.add,
             )
 
-        q_rows_of = []
+        def moments(t, q_rows):
+            for h in range(0, HEADS, 2):
+                nc.vector.bn_stats(
+                    out=q_stats[:, t, h : h + 2, :].rearrange("p h s -> p (h s)"),
+                    in_=q_rows[:, h * HEAD_DIM : (h + 2) * HEAD_DIM].rearrange("p (h d) -> p d h", h=2),
+                )
 
-        def square_q(t):
-            sums_of_squares(q_rows_of[t], q_sumsq[:, t * HEADS : (t + 1) * HEADS])
-
-        def after_q(t, q_sb):
-            q_rows_of.append(q_sb[:, t % PAIR, :])
-            if t >= SQUARES_LAG:
-                square_q(t - SQUARES_LAG)
-            if t >= PRODUCTS_LAG:
-                add_products(t - PRODUCTS_LAG)
-
-        def similarity():
-            nc.vector.tensor_mul(
-                out=denominator[:],
-                in0=denominator[:],
-                in1=g_norm_x4[:].unsqueeze(1).to_broadcast([P, TILES, HEADS]),
-            )
-            nc.vector.reciprocal(out=denominator[:], in_=denominator[:])
-            cosines = const.tile([P, TILES, HEADS], F32)
-            nc.vector.tensor_mul(
-                out=cosines[:], in0=q_dot_g[:].rearrange("p (t h) -> p t h", h=HEADS), in1=denominator[:]
-            )
-            sim = const.tile([P, TILES], F32)
-            nc.vector.tensor_reduce(out=sim[:], in_=cosines[:], axis=mybir.AxisListType.X, op=ALU.add)
-            first_row = const.tile([P, FIRST_ROW_RUNS, 2 * FIRST_ROW_RUN], F32)
-            nc.vector.tensor_copy(
-                out=first_row[0:1, :, 0:FIRST_ROW_RUN],
-                in_=sim[0:1, REGISTERS:TILES].rearrange("o (r c) -> o r c", c=FIRST_ROW_RUN),
-            )
-            whole_rows = out_3[0, TILES - REGISTERS : TOKENS - REGISTERS].rearrange("(p t) -> p t", t=TILES)
-            nc.sync.dma_start(out=whole_rows[0 : P // 2, :], in_=sim[1 : 1 + P // 2, :])
-            nc.sync.dma_start(out=whole_rows[P // 2 : P - 1, :], in_=sim[1 + P // 2 : P, :])
-            nc.sync.dma_start(
-                out=out_3[0:1, 0 : TILES - REGISTERS].rearrange("o (r c) -> o r c", c=FIRST_ROW_RUN),
-                in_=first_row[0:1, :, 0:FIRST_ROW_RUN],
-            )
-
+        transpose_next_pair()
         regroup_next_pair(nc.vector.tensor_copy)
         quantise_next_pair()
         g_bank = psum_acc.tile([P, WIDTH], F32, tag="acc2")
@@ -209,63 +170,84 @@ def tile_memeffattention_pa_t_kernel(tc, x, W_qkv_words, W_qkv_scales, q_g, out_
         nc.scalar.copy(out=g_all[:], in_=g_bank[:])
         g_sumsq = const.tile([P, HEADS], F32)
         g_norm_x4 = const.tile([P, HEADS], F32)
-        sums_of_squares(g_all, g_sumsq)
+        for h in range(HEADS):
+            squares = scrap.tile([P, HEAD_DIM], F32)
+            nc.scalar.activation(
+                out=squares[:],
+                in_=g_all[:, h * HEAD_DIM : (h + 1) * HEAD_DIM],
+                func=ACT.Square,
+                accum_out=g_sumsq[:, h : h + 1],
+            )
         nc.scalar.activation(out=g_norm_x4[:], in_=g_sumsq[:], func=ACT.Sqrt, scale=16.0)
+        transpose_next_pair()
         regroup_next_pair(nc.vector.tensor_copy)
-        denominator = const.tile([P, TILES, HEADS], F32)
-        for r in range(ROUNDS + 1):
-            with_q = r < ROUNDS
-            with_kv = r > 0
-            qa = ROUND * r
+
+        for j in range(PAIRS):
+            qa = PAIR * j
             ka = qa - PAIR
-            if r == ROUNDS:
-                for t in range(TILES - SQUARES_LAG, TILES):
-                    square_q(t)
-                nc.scalar.activation(
-                    out=denominator[:].rearrange("p t h -> p (t h)"), in_=q_sumsq[:], func=ACT.Sqrt
-                )
-                add_products(TILES - 2)
-            if with_q:
-                q_ab = results.tile([P, PAIR, WIDTH], F32, tag="q")
-                take_q(qa, q_ab)
-            if r == 0:
-                regroup_next_pair()
-            if with_kv:
+            if j > 0:
+                quantise_next_pair()
+            q_ab = results.tile([P, PAIR, WIDTH], F32, tag="q")
+            products = products_pool.tile([P, PAIR, HEADS, HEAD_DIM], F32)
+            products_of.append(products)
+            take(nc.scalar.copy, qa, 0, q_ab)
+            multiply_by_g(products, 0, q_ab)
+            take(nc.vector.tensor_copy, qa + 1, 0, q_ab)
+            multiply_by_g(products, 1, q_ab)
+            if j == 0:
+                quantise_next_pair()
+            transpose_next_pair()
+            moments(qa, q_ab[:, 0, :])
+            if j > 0:
                 k_ab = results.tile([P, PAIR, WIDTH], F32, tag="k")
                 v_ab = results.tile([P, PAIR, WIDTH], F32, tag="v")
-                take(nc.vector.tensor_copy, ka, 1, k_ab)
+                take(nc.scalar.copy, ka, 1, k_ab)
                 take(nc.scalar.copy, ka, 2, v_ab)
-            if with_q:
-                after_q(qa, q_ab)
-            if r == ROUNDS:
-                add_products(TILES - 1)
-            if with_kv:
-                take(nc.vector.tensor_copy if with_q else nc.scalar.copy, ka + 1, 1, k_ab)
-            quantise_next_pair()
-            if r > 0:
-                quantise_next_pair()
-            if with_q:
-                take_q(qa + 1, q_ab)
-            if r == 0:
-                quantise_next_pair()
-            if with_kv:
+                add_products(j - 1)
+            regroup_next_pair(nc.scalar.copy)
+            moments(qa + 1, q_ab[:, 1, :])
+            if j > 0:
+                take(nc.scalar.copy, ka + 1, 1, k_ab)
                 take(nc.scalar.copy, ka + 1, 2, v_ab)
-            if with_q:
-                after_q(qa + 1, q_ab)
-            regroup_next_pair()
-            if r == ROUNDS:
-                similarity()
 
-            if with_q:
-                q_cd = results.tile([P, PAIR, WIDTH], F32, tag="q")
-                k_cd = results.tile([P, PAIR, WIDTH], F32, tag="k")
-                v_cd = results.tile([P, PAIR, WIDTH], F32, tag="v")
-                take_q(qa + 2, q_cd)
-                take(nc.vector.tensor_copy, ka + 2, 1, k_cd)
-                take(nc.scalar.copy, ka + 2, 2, v_cd)
-                after_q(qa + 2, q_cd)
-                take_q(qa + 3, q_cd)
-                take(nc.scalar.copy, ka + 3, 1, k_cd)
-                take(nc.scalar.copy, ka + 3, 2, v_cd)
-                after_q(qa + 3, q_cd)
-                regroup_next_pair()
+        ka = TILES - PAIR
+        k_ab = results.tile([P, PAIR, WIDTH], F32, tag="k")
+        v_ab = results.tile([P, PAIR, WIDTH], F32, tag="v")
+        means = q_stats[:, :, :, 1]
+        spreads = q_stats[:, :, :, 2]
+        squared_norm = const.tile([P, TILES, HEADS], F32)
+        denominator = const.tile([P, TILES, HEADS], F32)
+        nc.vector.tensor_mul(out=squared_norm[:], in0=means, in1=means)
+        take(nc.scalar.copy, ka, 1, k_ab)
+        take(nc.scalar.copy, ka, 2, v_ab)
+        nc.vector.scalar_tensor_tensor(
+            out=squared_norm[:], in0=squared_norm[:], scalar=float(HEAD_DIM), in1=spreads, op0=ALU.mult, op1=ALU.add
+        )
+        nc.scalar.activation(out=denominator[:], in_=squared_norm[:], func=ACT.Sqrt)
+        add_products(PAIRS - 1)
+        take(nc.vector.tensor_copy, ka + 1, 1, k_ab)
+        take(nc.scalar.copy, ka + 1, 2, v_ab)
+        nc.vector.tensor_mul(
+            out=denominator[:],
+            in0=denominator[:],
+            in1=g_norm_x4[:].unsqueeze(1).to_broadcast([P, TILES, HEADS]),
+        )
+        nc.vector.reciprocal(out=denominator[:], in_=denominator[:])
+        cosines = const.tile([P, TILES, HEADS], F32)
+        nc.vector.tensor_mul(
+            out=cosines[:], in0=q_dot_g[:].rearrange("p (t h) -> p t h", h=HEADS), in1=denominator[:]
+        )
+        sim = const.tile([P, TILES], F32)
+        nc.vector.tensor_reduce(out=sim[:], in_=cosines[:], axis=mybir.AxisListType.X, op=ALU.add)
+        first_row = const.tile([P, FIRST_ROW_RUNS, 2 * FIRST_ROW_RUN], F32)
+        nc.vector.tensor_copy(
+            out=first_row[0:1, :, 0:FIRST_ROW_RUN],
+            in_=sim[0:1, REGISTERS:TILES].rearrange("o (r c) -> o r c", c=FIRST_ROW_RUN),
+        )
+        whole_rows = out_3[0, TILES - REGISTERS : TOKENS - REGISTERS].rearrange("(p t) -> p t", t=TILES)
+        nc.sync.dma_start(out=whole_rows[0 : P // 2, :], in_=sim[1 : 1 + P // 2, :])
+        nc.sync.dma_start(out=whole_rows[P // 2 : P - 1, :], in_=sim[1 + P // 2 : P, :])
+        nc.sync.dma_start(
+            out=out_3[0:1, 0 : TILES - REGISTERS].rearrange("o (r c) -> o r c", c=FIRST_ROW_RUN),
+            in_=first_row[0:1, :, 0:FIRST_ROW_RUN],
+        )

@@ -25,10 +25,14 @@ PAIR = 2
 PAIRS = TILES // PAIR
 WORDS = K // 2
 STATS = 3
-RESULT_BUFS = 12
+LOAD_TILES = [2] * 4 + [8] * 3
+STORE_TILES = ([2] * 2 + [4] * 7, [2] * 2 + [4] * 7, [2] + [4] * 7 + [2])
+RESULT_BUFS = 6
 WARM_UP = 3
 FIRST_ROW_RUNS = 3
 FIRST_ROW_RUN = (TILES - REGISTERS) // FIRST_ROW_RUNS
+
+STORE_STARTS = [{sum(sizes[:i]): tiles for i, tiles in enumerate(sizes)} for sizes in STORE_TILES]
 
 FLOPS = 2 * TOKENS * K * 3 * WIDTH
 
@@ -40,7 +44,7 @@ def tile_memeffattention_pa_t_kernel(tc, x, W_qkv_words, W_qkv_scales, q_g, out_
 
     with ExitStack() as ctx:
         const = ctx.enter_context(tc.tile_pool(name="const", bufs=1))
-        x_pool = ctx.enter_context(tc.tile_pool(name="x_pool", bufs=PAIRS))
+        x_pool = ctx.enter_context(tc.tile_pool(name="x_pool", bufs=1))
         prep = ctx.enter_context(tc.tile_pool(name="prep", bufs=4))
         quantised = ctx.enter_context(tc.tile_pool(name="quantised", bufs=6))
         results = ctx.enter_context(tc.tile_pool(name="results", bufs=RESULT_BUFS))
@@ -69,12 +73,15 @@ def tile_memeffattention_pa_t_kernel(tc, x, W_qkv_words, W_qkv_scales, q_g, out_
         nc.vector.memset(one[:], 1.0)
         nc.scalar.activation(out=one[:], in_=one[:], func=ACT.Sqrt)
 
-        def load_x(j):
-            x_sb = x_pool.tile([P, PAIR, K], BF16)
-            nc.sync.dma_start(out=x_sb[:], in_=x_tiles[:, j * PAIR : (j + 1) * PAIR, :])
-            return x_sb
+        x_rows_of = []
 
-        x_loaded = [load_x(0)]
+        def load_x(tiles):
+            first = len(x_rows_of)
+            x_sb = x_pool.tile([P, tiles, K], BF16, name="x_%d" % first)
+            nc.sync.dma_start(out=x_sb[:], in_=x_tiles[:, first : first + tiles, :])
+            x_rows_of.extend([x_sb[:, i, :] for i in range(tiles)])
+
+        load_x(LOAD_TILES[0])
         w_words = const.tile([P, 2 * 3 * WIDTH], U8, align_bytes=64)
         nc.sync.dma_start(out=w_words[:].bitcast(I32), in_=W_qkv_words[0].bitcast(I32))
         for quadrant in range(4):
@@ -82,7 +89,8 @@ def tile_memeffattention_pa_t_kernel(tc, x, W_qkv_words, W_qkv_scales, q_g, out_
                 out=w_scales[32 * quadrant : 32 * quadrant + 4, :].bitcast(I32),
                 in_=W_qkv_scales[0, 4 * quadrant : 4 * quadrant + 4, :].bitcast(I32),
             )
-        x_loaded.extend([load_x(j) for j in range(1, PAIRS)])
+        for tiles in LOAD_TILES[1:]:
+            load_x(tiles)
 
         q_stats = const.tile([P, TILES, HEADS, STATS], F32)
         q_dot_g = const.tile([P, TILES * HEADS], F32)
@@ -98,7 +106,7 @@ def tile_memeffattention_pa_t_kernel(tc, x, W_qkv_words, W_qkv_scales, q_g, out_
                 return
             xt = psum_xt.tile([P, PAIR, 2, P], F32)
             for i in range(PAIR):
-                words = x_loaded[j][:, i, :].bitcast(F32)
+                words = x_rows_of[j * PAIR + i].bitcast(F32)
                 for u in range(2):
                     nc.tensor.transpose(xt[:, i, u, :], words[:, u:WORDS:2], identity[:])
             transposed_pairs.append(xt)
@@ -123,7 +131,15 @@ def tile_memeffattention_pa_t_kernel(tc, x, W_qkv_words, W_qkv_scales, q_g, out_
             nc.vector.quantize_mx(out=codes[:].bitcast(FP8X4), scales=scales[:], in_=grouped_pairs[j][:])
             quantised_pairs.append((codes, scales))
 
-        def take(copy, t, o, result):
+        rows_of = [[], [], []]
+        filling = [None, None, None]
+
+        def take(copy, t, o):
+            if t in STORE_STARTS[o]:
+                group = results.tile([P, STORE_STARTS[o][t], WIDTH], F32, name="out%d" % o, tag="out%d" % o)
+                filling[o] = (group, t)
+            group, first = filling[o]
+            rows_of[o].append(group[:, t - first, :])
             j, i = divmod(t, PAIR)
             codes, scales = quantised_pairs[j]
             tokens = slice(i * P, (i + 1) * P)
@@ -137,13 +153,13 @@ def tile_memeffattention_pa_t_kernel(tc, x, W_qkv_words, W_qkv_scales, q_g, out_
                 start=True,
                 stop=True,
             )
-            copy(out=result[:, i, :], in_=acc[:])
-            if i == PAIR - 1:
-                nc.sync.dma_start(out=qkv_tiles[o][:, PAIR * j : PAIR * (j + 1), :], in_=result[:])
+            copy(out=rows_of[o][t], in_=acc[:])
+            if t + 1 == first + STORE_STARTS[o][first]:
+                nc.sync.dma_start(out=qkv_tiles[o][:, first : t + 1, :], in_=group[:])
 
-        def multiply_by_g(products, i, q_ab):
+        def multiply_by_g(products, t):
             nc.gpsimd.tensor_mul(
-                out=products[:, i, :, :].rearrange("p h d -> p (h d)"), in0=q_ab[:, i, :], in1=g_all[:]
+                out=products[:, t % PAIR, :, :].rearrange("p h d -> p (h d)"), in0=rows_of[0][t], in1=g_all[:]
             )
 
         def add_products(j):
@@ -154,11 +170,11 @@ def tile_memeffattention_pa_t_kernel(tc, x, W_qkv_words, W_qkv_scales, q_g, out_
                 op=ALU.add,
             )
 
-        def moments(t, q_rows):
+        def moments(t):
             for h in range(0, HEADS, 2):
                 nc.vector.bn_stats(
                     out=q_stats[:, t, h : h + 2, :].rearrange("p h s -> p (h s)"),
-                    in_=q_rows[:, h * HEAD_DIM : (h + 2) * HEAD_DIM].rearrange("p (h d) -> p d h", h=2),
+                    in_=rows_of[0][t][:, h * HEAD_DIM : (h + 2) * HEAD_DIM].rearrange("p (h d) -> p d h", h=2),
                 )
 
         transpose_next_pair()
@@ -187,46 +203,41 @@ def tile_memeffattention_pa_t_kernel(tc, x, W_qkv_words, W_qkv_scales, q_g, out_
             ka = qa - PAIR
             if j > 0:
                 quantise_next_pair()
-            q_ab = results.tile([P, PAIR, WIDTH], F32, tag="q")
             products = products_pool.tile([P, PAIR, HEADS, HEAD_DIM], F32)
             products_of.append(products)
-            take(nc.scalar.copy, qa, 0, q_ab)
-            multiply_by_g(products, 0, q_ab)
-            take(nc.vector.tensor_copy, qa + 1, 0, q_ab)
-            multiply_by_g(products, 1, q_ab)
+            take(nc.scalar.copy, qa, 0)
+            multiply_by_g(products, qa)
+            take(nc.vector.tensor_copy, qa + 1, 0)
+            multiply_by_g(products, qa + 1)
             if j == 0:
                 quantise_next_pair()
             transpose_next_pair()
-            moments(qa, q_ab[:, 0, :])
+            moments(qa)
             if j > 0:
-                k_ab = results.tile([P, PAIR, WIDTH], F32, tag="k")
-                v_ab = results.tile([P, PAIR, WIDTH], F32, tag="v")
-                take(nc.scalar.copy, ka, 1, k_ab)
-                take(nc.scalar.copy, ka, 2, v_ab)
+                take(nc.scalar.copy, ka, 1)
+                take(nc.scalar.copy, ka, 2)
                 add_products(j - 1)
             regroup_next_pair(nc.scalar.copy)
-            moments(qa + 1, q_ab[:, 1, :])
+            moments(qa + 1)
             if j > 0:
-                take(nc.scalar.copy, ka + 1, 1, k_ab)
-                take(nc.scalar.copy, ka + 1, 2, v_ab)
+                take(nc.scalar.copy, ka + 1, 1)
+                take(nc.scalar.copy, ka + 1, 2)
 
         ka = TILES - PAIR
-        k_ab = results.tile([P, PAIR, WIDTH], F32, tag="k")
-        v_ab = results.tile([P, PAIR, WIDTH], F32, tag="v")
         means = q_stats[:, :, :, 1]
         spreads = q_stats[:, :, :, 2]
         squared_norm = const.tile([P, TILES, HEADS], F32)
         denominator = const.tile([P, TILES, HEADS], F32)
         nc.vector.tensor_mul(out=squared_norm[:], in0=means, in1=means)
-        take(nc.scalar.copy, ka, 1, k_ab)
-        take(nc.scalar.copy, ka, 2, v_ab)
+        take(nc.scalar.copy, ka, 1)
+        take(nc.scalar.copy, ka, 2)
         nc.vector.scalar_tensor_tensor(
             out=squared_norm[:], in0=squared_norm[:], scalar=float(HEAD_DIM), in1=spreads, op0=ALU.mult, op1=ALU.add
         )
         nc.scalar.activation(out=denominator[:], in_=squared_norm[:], func=ACT.Sqrt)
         add_products(PAIRS - 1)
-        take(nc.vector.tensor_copy, ka + 1, 1, k_ab)
-        take(nc.scalar.copy, ka + 1, 2, v_ab)
+        take(nc.vector.tensor_copy, ka + 1, 1)
+        take(nc.scalar.copy, ka + 1, 2)
         nc.vector.tensor_mul(
             out=denominator[:],
             in0=denominator[:],

@@ -26,7 +26,7 @@ PAIRS = TILES // PAIR
 WORDS = K // 2
 STATS = 3
 LOAD_TILES = [2] * 4 + [8] * 3
-STORE_TILES = ([2] * 2 + [4] * 7, [2] * 2 + [4] * 7, [2] + [4] * 7 + [2])
+STORE_TILES = ([2] * 2 + [4] * 7, [2] + [4] * 7 + [2], [2] * 2 + [4] * 7)
 RESULT_BUFS = 6
 WARM_UP = 3
 FIRST_ROW_RUNS = 3
@@ -48,7 +48,6 @@ def tile_memeffattention_pa_t_kernel(tc, x, W_qkv_words, W_qkv_scales, q_g, out_
         prep = ctx.enter_context(tc.tile_pool(name="prep", bufs=4))
         quantised = ctx.enter_context(tc.tile_pool(name="quantised", bufs=6))
         results = ctx.enter_context(tc.tile_pool(name="results", bufs=RESULT_BUFS))
-        scrap = ctx.enter_context(tc.tile_pool(name="scrap", bufs=2))
         products_pool = ctx.enter_context(tc.tile_pool(name="products_pool", bufs=3))
         psum_xt = ctx.enter_context(tc.psum_pool(name="psum_xt", bufs=2))
         psum_acc = ctx.enter_context(tc.psum_pool(name="psum_acc", bufs=2))
@@ -92,7 +91,7 @@ def tile_memeffattention_pa_t_kernel(tc, x, W_qkv_words, W_qkv_scales, q_g, out_
         for tiles in LOAD_TILES[1:]:
             load_x(tiles)
 
-        q_stats = const.tile([P, TILES, HEADS, STATS], F32)
+        stats = const.tile([P, TILES + 1, HEADS, STATS], F32)
         q_dot_g = const.tile([P, TILES * HEADS], F32)
 
         transposed_pairs = []
@@ -157,9 +156,14 @@ def tile_memeffattention_pa_t_kernel(tc, x, W_qkv_words, W_qkv_scales, q_g, out_
             if t + 1 == first + STORE_STARTS[o][first]:
                 nc.sync.dma_start(out=qkv_tiles[o][:, first : t + 1, :], in_=group[:])
 
-        def multiply_by_g(products, t):
+        def begin_products():
+            products = products_pool.tile([P, PAIR, HEADS, HEAD_DIM], F32)
+            products_of.append(products)
+
+        def multiply_by_g(t):
+            j, i = divmod(t, PAIR)
             nc.gpsimd.tensor_mul(
-                out=products[:, t % PAIR, :, :].rearrange("p h d -> p (h d)"), in0=rows_of[0][t], in1=g_all[:]
+                out=products_of[j][:, i, :, :].rearrange("p h d -> p (h d)"), in0=rows_of[0][t], in1=g_all[:]
             )
 
         def add_products(j):
@@ -170,11 +174,11 @@ def tile_memeffattention_pa_t_kernel(tc, x, W_qkv_words, W_qkv_scales, q_g, out_
                 op=ALU.add,
             )
 
-        def moments(t):
+        def moments(rows, t):
             for h in range(0, HEADS, 2):
                 nc.vector.bn_stats(
-                    out=q_stats[:, t, h : h + 2, :].rearrange("p h s -> p (h s)"),
-                    in_=rows_of[0][t][:, h * HEAD_DIM : (h + 2) * HEAD_DIM].rearrange("p (h d) -> p d h", h=2),
+                    out=stats[:, t, h : h + 2, :].rearrange("p h s -> p (h s)"),
+                    in_=rows[:, h * HEAD_DIM : (h + 2) * HEAD_DIM].rearrange("p (h d) -> p d h", h=2),
                 )
 
         transpose_next_pair()
@@ -184,66 +188,71 @@ def tile_memeffattention_pa_t_kernel(tc, x, W_qkv_words, W_qkv_scales, q_g, out_
         nc.tensor.matmul(out=g_bank[:], lhsT=ones[:], rhs=g_rows[:], start=True, stop=True)
         g_all = const.tile([P, WIDTH], F32)
         nc.scalar.copy(out=g_all[:], in_=g_bank[:])
-        g_sumsq = const.tile([P, HEADS], F32)
-        g_norm_x4 = const.tile([P, HEADS], F32)
-        for h in range(HEADS):
-            squares = scrap.tile([P, HEAD_DIM], F32)
-            nc.scalar.activation(
-                out=squares[:],
-                in_=g_all[:, h * HEAD_DIM : (h + 1) * HEAD_DIM],
-                func=ACT.Square,
-                accum_out=g_sumsq[:, h : h + 1],
-            )
-        nc.scalar.activation(out=g_norm_x4[:], in_=g_sumsq[:], func=ACT.Sqrt, scale=16.0)
         transpose_next_pair()
         regroup_next_pair(nc.vector.tensor_copy)
 
-        for j in range(PAIRS):
-            qa = PAIR * j
-            ka = qa - PAIR
+        copy_s = nc.scalar.copy
+        copy_v = nc.vector.tensor_copy
+        last = PAIRS - 1
+        for j in range(last):
+            a = PAIR * j
+            b = a + 1
             if j > 0:
                 quantise_next_pair()
-            products = products_pool.tile([P, PAIR, HEADS, HEAD_DIM], F32)
-            products_of.append(products)
-            take(nc.scalar.copy, qa, 0)
-            multiply_by_g(products, qa)
-            take(nc.vector.tensor_copy, qa + 1, 0)
-            multiply_by_g(products, qa + 1)
+            begin_products()
+            take(copy_s, a, 0)
+            multiply_by_g(a)
+            take(copy_v, b, 0)
+            multiply_by_g(b)
             if j == 0:
                 quantise_next_pair()
             transpose_next_pair()
-            moments(qa)
+            moments(rows_of[0][a], a)
+            take(copy_s, a, 1)
+            take(copy_s, a, 2)
             if j > 0:
-                take(nc.scalar.copy, ka, 1)
-                take(nc.scalar.copy, ka, 2)
                 add_products(j - 1)
-            regroup_next_pair(nc.scalar.copy)
-            moments(qa + 1)
-            if j > 0:
-                take(nc.scalar.copy, ka + 1, 1)
-                take(nc.scalar.copy, ka + 1, 2)
+            else:
+                moments(g_all, TILES)
+            regroup_next_pair(copy_s)
+            moments(rows_of[0][b], b)
+            if j < last - 1:
+                take(copy_s, b, 1)
+                take(copy_s, b, 2)
 
-        ka = TILES - PAIR
-        means = q_stats[:, :, :, 1]
-        spreads = q_stats[:, :, :, 2]
-        squared_norm = const.tile([P, TILES, HEADS], F32)
-        denominator = const.tile([P, TILES, HEADS], F32)
-        nc.vector.tensor_mul(out=squared_norm[:], in0=means, in1=means)
-        take(nc.scalar.copy, ka, 1)
-        take(nc.scalar.copy, ka, 2)
+        a = PAIR * last
+        b = a + 1
+        begin_products()
+        quantise_next_pair()
+        take(copy_s, a, 0)
+        multiply_by_g(a)
+        take(copy_s, b, 0)
+        multiply_by_g(b)
+        moments(rows_of[0][a], a)
+        take(copy_s, a - 1, 1)
+        take(copy_s, a - 1, 2)
+        moments(rows_of[0][b], b)
+        means = stats[:, :, :, 1]
+        spreads = stats[:, :, :, 2]
+        norms = const.tile([P, TILES + 1, HEADS], F32)
+        nc.vector.tensor_mul(out=norms[:], in0=means, in1=means)
+        take(copy_s, a, 1)
         nc.vector.scalar_tensor_tensor(
-            out=squared_norm[:], in0=squared_norm[:], scalar=float(HEAD_DIM), in1=spreads, op0=ALU.mult, op1=ALU.add
+            out=norms[:], in0=norms[:], scalar=float(HEAD_DIM), in1=spreads, op0=ALU.mult, op1=ALU.add
         )
-        nc.scalar.activation(out=denominator[:], in_=squared_norm[:], func=ACT.Sqrt)
-        add_products(PAIRS - 1)
-        take(nc.vector.tensor_copy, ka + 1, 1)
-        take(nc.scalar.copy, ka + 1, 2)
+        take(copy_s, a, 2)
+        add_products(last - 1)
+        nc.scalar.activation(out=norms[:], in_=norms[:], func=ACT.Sqrt, scale=4.0)
+        take(copy_s, b, 1)
+        denominator = const.tile([P, TILES, HEADS], F32)
         nc.vector.tensor_mul(
             out=denominator[:],
-            in0=denominator[:],
-            in1=g_norm_x4[:].unsqueeze(1).to_broadcast([P, TILES, HEADS]),
+            in0=norms[:, 0:TILES, :],
+            in1=norms[:, TILES : TILES + 1, :].to_broadcast([P, TILES, HEADS]),
         )
+        take(copy_s, b, 2)
         nc.vector.reciprocal(out=denominator[:], in_=denominator[:])
+        add_products(last)
         cosines = const.tile([P, TILES, HEADS], F32)
         nc.vector.tensor_mul(
             out=cosines[:], in0=q_dot_g[:].rearrange("p (t h) -> p t h", h=HEADS), in1=denominator[:]

@@ -25,7 +25,7 @@ PAIR = 2
 PAIRS = TILES // PAIR
 WORDS = K // 2
 STATS = 3
-LOAD_TILES = [2] * 4 + [8] * 3
+LOAD_TILES = [2, 2, 4, 8, 16]
 STORE_TILES = ([2] * 2 + [4] * 7, [2] + [4] * 7 + [2], [2] * 2 + [4] * 7)
 RESULT_BUFS = 6
 WARM_UP = 3
@@ -265,9 +265,9 @@ def tile_memeffattention_pa_t_kernel(tc, x, W_qkv_words, W_qkv_scales, q_g, out_
             in_=sim[0:1, REGISTERS:TILES].rearrange("o (r c) -> o r c", c=FIRST_ROW_RUN),
         )
         whole_rows = out_3[0, TILES - REGISTERS : TOKENS - REGISTERS].rearrange("(p t) -> p t", t=TILES)
-        nc.sync.dma_start(out=whole_rows[0 : P // 2, :], in_=sim[1 : 1 + P // 2, :])
-        nc.sync.dma_start(out=whole_rows[P // 2 : P - 1, :], in_=sim[1 + P // 2 : P, :])
-        nc.sync.dma_start(
+        nc.scalar.dma_start(out=whole_rows[0 : P // 2, :], in_=sim[1 : 1 + P // 2, :])
+        nc.scalar.dma_start(out=whole_rows[P // 2 : P - 1, :], in_=sim[1 + P // 2 : P, :])
+        nc.scalar.dma_start(
             out=out_3[0:1, 0 : TILES - REGISTERS].rearrange("o (r c) -> o r c", c=FIRST_ROW_RUN),
             in_=first_row[0:1, :, 0:FIRST_ROW_RUN],
         )

@@ -70,7 +70,7 @@ def tile_memeffattention_pa_t_kernel(tc, x, W_qkv_words, W_qkv_scales, q_g, out_
 
         one = const.tile([P, 1], F32)
         nc.vector.memset(one[:], 1.0)
-        nc.scalar.activation(out=one[:], in_=one[:], func=ACT.Sqrt)
+        nc.scalar.activation(out=one[:], in_=one[:], func=ACT.Abs_reciprocal_sqrt)
 
         x_rows_of = []
 
@@ -242,20 +242,19 @@ def tile_memeffattention_pa_t_kernel(tc, x, W_qkv_words, W_qkv_scales, q_g, out_
         )
         take(copy_s, a, 2)
         add_products(last - 1)
-        nc.scalar.activation(out=norms[:], in_=norms[:], func=ACT.Sqrt, scale=4.0)
+        nc.scalar.activation(out=norms[:], in_=norms[:], func=ACT.Abs_reciprocal_sqrt, scale=4.0)
         take(copy_s, b, 1)
-        denominator = const.tile([P, TILES, HEADS], F32)
-        nc.vector.tensor_mul(
-            out=denominator[:],
+        factors = const.tile([P, TILES, HEADS], F32)
+        nc.gpsimd.tensor_mul(
+            out=factors[:],
             in0=norms[:, 0:TILES, :],
             in1=norms[:, TILES : TILES + 1, :].to_broadcast([P, TILES, HEADS]),
         )
         take(copy_s, b, 2)
-        nc.vector.reciprocal(out=denominator[:], in_=denominator[:])
         add_products(last)
         cosines = const.tile([P, TILES, HEADS], F32)
         nc.vector.tensor_mul(
-            out=cosines[:], in0=q_dot_g[:].rearrange("p (t h) -> p t h", h=HEADS), in1=denominator[:]
+            out=cosines[:], in0=q_dot_g[:].rearrange("p (t h) -> p t h", h=HEADS), in1=factors[:]
         )
         sim = const.tile([P, TILES], F32)
         nc.vector.tensor_reduce(out=sim[:], in_=cosines[:], axis=mybir.AxisListType.X, op=ALU.add)

@@ -74,13 +74,13 @@ def tile_memeffattention_pa_t_kernel(tc, x, W_qkv_words, W_qkv_scales, q_g, out_
 
         x_rows_of = []
 
-        def load_x(tiles):
+        def load_x(tiles, queue):
             first = len(x_rows_of)
             x_sb = x_pool.tile([P, tiles, K], BF16, name="x_%d" % first)
-            nc.sync.dma_start(out=x_sb[:], in_=x_tiles[:, first : first + tiles, :])
+            queue.dma_start(out=x_sb[:], in_=x_tiles[:, first : first + tiles, :])
             x_rows_of.extend([x_sb[:, i, :] for i in range(tiles)])
 
-        load_x(LOAD_TILES[0])
+        load_x(LOAD_TILES[0], nc.sync)
         w_words = const.tile([P, 2 * 3 * WIDTH], U8, align_bytes=64)
         nc.sync.dma_start(out=w_words[:].bitcast(I32), in_=W_qkv_words[0].bitcast(I32))
         for quadrant in range(4):
@@ -88,8 +88,8 @@ def tile_memeffattention_pa_t_kernel(tc, x, W_qkv_words, W_qkv_scales, q_g, out_
                 out=w_scales[32 * quadrant : 32 * quadrant + 4, :].bitcast(I32),
                 in_=W_qkv_scales[0, 4 * quadrant : 4 * quadrant + 4, :].bitcast(I32),
             )
-        for tiles in LOAD_TILES[1:]:
-            load_x(tiles)
+        for tiles in LOAD_TILES[1:-1]:
+            load_x(tiles, nc.sync)
 
         stats = const.tile([P, TILES + 1, HEADS, STATS], F32)
         q_dot_g = const.tile([P, TILES * HEADS], F32)
@@ -188,6 +188,7 @@ def tile_memeffattention_pa_t_kernel(tc, x, W_qkv_words, W_qkv_scales, q_g, out_
         nc.tensor.matmul(out=g_bank[:], lhsT=ones[:], rhs=g_rows[:], start=True, stop=True)
         g_all = const.tile([P, WIDTH], F32)
         nc.scalar.copy(out=g_all[:], in_=g_bank[:])
+        load_x(LOAD_TILES[-1], nc.scalar)
         transpose_next_pair()
         regroup_next_pair(nc.vector.tensor_copy)
 

from contextlib import ExitStack

import concourse.mybir as mybir
from concourse.masks import make_identity

F32 = mybir.dt.float32
BF16 = mybir.dt.bfloat16
I32 = mybir.dt.int32
U32 = mybir.dt.uint32
U8 = mybir.dt.uint8
FP8X4 = mybir.dt.float8_e4m3fn_x4
FP4X4 = mybir.dt.float4_e2m1fn_x4
ACT = mybir.ActivationFunctionType
ALU = mybir.AluOpType

P = 128
TOKENS = 4096
K = 512
HEADS = 4
HEAD_DIM = 128
WIDTH = HEADS * HEAD_DIM
REGISTERS = 5
TILES = TOKENS // P
PAIR = 2
PAIRS = TILES // PAIR
WORDS = K // 2
STATS = 3
LOAD_TILES = [2, 2, 4, 8, 16]
STORE_TILES = ([2] * 2 + [4] * 7, [2] + [4] * 7 + [2], [2] * 2 + [4] * 7)
RESULT_BUFS = 6
WARM_UP = 3
FIRST_ROW_RUNS = 3
FIRST_ROW_RUN = (TILES - REGISTERS) // FIRST_ROW_RUNS

STORE_STARTS = [{sum(sizes[:i]): tiles for i, tiles in enumerate(sizes)} for sizes in STORE_TILES]

FLOPS = 2 * TOKENS * K * 3 * WIDTH


def tile_memeffattention_pa_t_kernel(tc, x, W_qkv_words, W_qkv_scales, q_g, out_0, out_1, out_2, out_3):
    nc = tc.nc
    x_tiles = x[0].rearrange("(p t) c -> p t c", t=TILES)
    qkv_tiles = [o[0].rearrange("(p t) h d -> p t (h d)", t=TILES) for o in (out_0, out_1, out_2)]

    with ExitStack() as ctx:
        const = ctx.enter_context(tc.tile_pool(name="const", bufs=1))
        x_pool = ctx.enter_context(tc.tile_pool(name="x_pool", bufs=1))
        prep = ctx.enter_context(tc.tile_pool(name="prep", bufs=4))
        quantised = ctx.enter_context(tc.tile_pool(name="quantised", bufs=6))
        results = ctx.enter_context(tc.tile_pool(name="results", bufs=RESULT_BUFS))
        products_pool = ctx.enter_context(tc.tile_pool(name="products_pool", bufs=3))
        psum_xt = ctx.enter_context(tc.psum_pool(name="psum_xt", bufs=2))
        psum_acc = ctx.enter_context(tc.psum_pool(name="psum_acc", bufs=2))
        ctx.enter_context(tc.manual_schedule())

        zeros = const.tile([P, WIDTH], BF16)
        nc.gpsimd.memset(zeros[:], 0.0)
        warm_bank = psum_acc.tile([P, WIDTH], F32, tag="acc1")
        for i in range(WARM_UP):
            nc.tensor.matmul(out=warm_bank[:], lhsT=zeros[:, 0:P], rhs=zeros[:], start=True, stop=True)
        g_rows = const.tile([P, WIDTH], BF16)
        nc.vector.memset(g_rows[:], 0.0)
        nc.scalar.dma_start(out=g_rows[0:1, :], in_=q_g.rearrange("(o h) d -> o (h d)", o=1))
        w_scales = const.tile([P, 3 * WIDTH], U8, align_bytes=64)
        nc.vector.memset(w_scales[:].bitcast(I32), 0)
        ones = const.tile([P, P], BF16)
        nc.vector.memset(ones[:], 1.0)
        identity = const.tile([P, P], F32)
        make_identity(nc, identity[:])

        one = const.tile([P, 1], F32)
        nc.vector.memset(one[:], 1.0)
        nc.scalar.activation(out=one[:], in_=one[:], func=ACT.Abs_reciprocal_sqrt)

        x_rows_of = []

        def load_x(tiles, queue):
            first = len(x_rows_of)
            x_sb = x_pool.tile([P, tiles, K], BF16, name="x_%d" % first)
            queue.dma_start(out=x_sb[:], in_=x_tiles[:, first : first + tiles, :])
            x_rows_of.extend([x_sb[:, i, :] for i in range(tiles)])

        load_x(LOAD_TILES[0], nc.sync)
        w_words = const.tile([P, 2 * 3 * WIDTH], U8, align_bytes=64)
        nc.sync.dma_start(out=w_words[:].bitcast(I32), in_=W_qkv_words[0].bitcast(I32))
        for quadrant in range(4):
            nc.sync.dma_start(
                out=w_scales[32 * quadrant : 32 * quadrant + 4, :].bitcast(I32),
                in_=W_qkv_scales[0, 4 * quadrant : 4 * quadrant + 4, :].bitcast(I32),
            )
        for tiles in LOAD_TILES[1:-1]:
            load_x(tiles, nc.sync)

        stats = const.tile([P, TILES + 1, HEADS, STATS], F32)
        q_dot_g = const.tile([P, TILES * HEADS], F32)

        transposed_pairs = []
        grouped_pairs = []
        quantised_pairs = []
        products_of = []

        def transpose_next_pair():
            j = len(transposed_pairs)
            if j == PAIRS:
                return
            xt = psum_xt.tile([P, PAIR, 2, P], F32)
            for i in range(PAIR):
                words = x_rows_of[j * PAIR + i].bitcast(F32)
                for u in range(2):
                    nc.tensor.transpose(xt[:, i, u, :], words[:, u:WORDS:2], identity[:])
            transposed_pairs.append(xt)

        def regroup_next_pair(copy):
            j = len(grouped_pairs)
            if j == PAIRS:
                return
            grouped = prep.tile([P, PAIR * P * 4], BF16, align_bytes=64)
            copy(
                out=grouped[:].bitcast(F32).rearrange("p (i r u) -> p i r u", i=PAIR, u=2),
                in_=transposed_pairs[j][:].rearrange("p i u r -> p i r u"),
            )
            grouped_pairs.append(grouped)

        def quantise_next_pair():
            j = len(quantised_pairs)
            if j == PAIRS:
                return
            codes = quantised.tile([P, PAIR * P], U32, align_bytes=64)
            scales = quantised.tile([P, PAIR * P], U8, align_bytes=64)
            nc.vector.quantize_mx(out=codes[:].bitcast(FP8X4), scales=scales[:], in_=grouped_pairs[j][:])
            quantised_pairs.append((codes, scales))

        rows_of = [[], [], []]
        filling = [None, None, None]

        def take(copy, t, o):
            if t in STORE_STARTS[o]:
                group = results.tile([P, STORE_STARTS[o][t], WIDTH], F32, name="out%d" % o, tag="out%d" % o)
                filling[o] = (group, t)
            group, first = filling[o]
            rows_of[o].append(group[:, t - first, :])
            j, i = divmod(t, PAIR)
            codes, scales = quantised_pairs[j]
            tokens = slice(i * P, (i + 1) * P)
            acc = psum_acc.tile([P, WIDTH], F32, name="acc%d" % o, tag="acc%d" % o)
            nc.tensor.matmul_mx(
                out=acc[:],
                lhsT=codes[:, tokens].bitcast(FP8X4),
                lhsT_scale=scales[:, tokens],
                rhs=w_words[:, 2 * o * WIDTH : 2 * (o + 1) * WIDTH].bitcast(FP4X4),
                rhs_scale=w_scales[:, o * WIDTH : (o + 1) * WIDTH],
                start=True,
                stop=True,
            )
            copy(out=rows_of[o][t], in_=acc[:])
            if t + 1 == first + STORE_STARTS[o][first]:
                nc.sync.dma_start(out=qkv_tiles[o][:, first : t + 1, :], in_=group[:])

        def begin_products():
            products = products_pool.tile([P, PAIR, HEADS, HEAD_DIM], F32)
            products_of.append(products)

        def multiply_by_g(t):
            j, i = divmod(t, PAIR)
            nc.gpsimd.tensor_mul(
                out=products_of[j][:, i, :, :].rearrange("p h d -> p (h d)"), in0=rows_of[0][t], in1=g_all[:]
            )

        def add_products(j):
            nc.vector.tensor_reduce(
                out=q_dot_g[:, j * PAIR * HEADS : (j + 1) * PAIR * HEADS],
                in_=products_of[j][:].rearrange("p i h d -> p (i h) d"),
                axis=mybir.AxisListType.X,
                op=ALU.add,
            )

        def moments(rows, t):
            for h in range(0, HEADS, 2):
                nc.vector.bn_stats(
                    out=stats[:, t, h : h + 2, :].rearrange("p h s -> p (h s)"),
                    in_=rows[:, h * HEAD_DIM : (h + 2) * HEAD_DIM].rearrange("p (h d) -> p d h", h=2),
                )

        transpose_next_pair()
        regroup_next_pair(nc.vector.tensor_copy)
        quantise_next_pair()
        g_bank = psum_acc.tile([P, WIDTH], F32, tag="acc2")
        nc.tensor.matmul(out=g_bank[:], lhsT=ones[:], rhs=g_rows[:], start=True, stop=True)
        g_all = const.tile([P, WIDTH], F32)
        nc.scalar.copy(out=g_all[:], in_=g_bank[:])
        load_x(LOAD_TILES[-1], nc.scalar)
        transpose_next_pair()
        regroup_next_pair(nc.vector.tensor_copy)

        copy_s = nc.scalar.copy
        copy_v = nc.vector.tensor_copy
        last = PAIRS - 1
        for j in range(last):
            a = PAIR * j
            b = a + 1
            if j > 0:
                quantise_next_pair()
            begin_products()
            take(copy_s, a, 0)
            multiply_by_g(a)
            take(copy_v, b, 0)
            multiply_by_g(b)
            if j == 0:
                quantise_next_pair()
            transpose_next_pair()
            moments(rows_of[0][a], a)
            take(copy_s, a, 1)
            take(copy_s, a, 2)
            if j > 0:
                add_products(j - 1)
            else:
                moments(g_all, TILES)
            regroup_next_pair(copy_s)
            moments(rows_of[0][b], b)
            if j < last - 1:
                take(copy_s, b, 1)
                take(copy_s, b, 2)

        a = PAIR * last
        b = a + 1
        begin_products()
        quantise_next_pair()
        take(copy_s, a, 0)
        multiply_by_g(a)
        take(copy_s, b, 0)
        multiply_by_g(b)
        moments(rows_of[0][a], a)
        take(copy_s, a - 1, 1)
        take(copy_s, a - 1, 2)
        moments(rows_of[0][b], b)
        means = stats[:, :, :, 1]
        spreads = stats[:, :, :, 2]
        norms = const.tile([P, TILES + 1, HEADS], F32)
        nc.vector.tensor_mul(out=norms[:], in0=means, in1=means)
        take(copy_s, a, 1)
        nc.vector.scalar_tensor_tensor(
            out=norms[:], in0=norms[:], scalar=float(HEAD_DIM), in1=spreads, op0=ALU.mult, op1=ALU.add
        )
        take(copy_s, a, 2)
        add_products(last - 1)
        nc.scalar.activation(out=norms[:], in_=norms[:], func=ACT.Abs_reciprocal_sqrt, scale=4.0)
        take(copy_s, b, 1)
        factors = const.tile([P, TILES, HEADS], F32)
        nc.gpsimd.tensor_mul(
            out=factors[:],
            in0=norms[:, 0:TILES, :],
            in1=norms[:, TILES : TILES + 1, :].to_broadcast([P, TILES, HEADS]),
        )
        take(copy_s, b, 2)
        add_products(last)
        cosines = const.tile([P, TILES, HEADS], F32)
        nc.vector.tensor_mul(
            out=cosines[:], in0=q_dot_g[:].rearrange("p (t h) -> p t h", h=HEADS), in1=factors[:]
        )
        sim = const.tile([P, TILES], F32)
        nc.vector.tensor_reduce(out=sim[:], in_=cosines[:], axis=mybir.AxisListType.X, op=ALU.add)
        first_row = const.tile([P, FIRST_ROW_RUNS, 2 * FIRST_ROW_RUN], F32)
        nc.vector.tensor_copy(
            out=first_row[0:1, :, 0:FIRST_ROW_RUN],
            in_=sim[0:1, REGISTERS:TILES].rearrange("o (r c) -> o r c", c=FIRST_ROW_RUN),
        )
        whole_rows = out_3[0, TILES - REGISTERS : TOKENS - REGISTERS].rearrange("(p t) -> p t", t=TILES)
        nc.scalar.dma_start(out=whole_rows[0 : P // 2, :], in_=sim[1 : 1 + P // 2, :])
        nc.scalar.dma_start(out=whole_rows[P // 2 : P - 1, :], in_=sim[1 + P // 2 : P, :])
        nc.scalar.dma_start(
            out=out_3[0:1, 0 : TILES - REGISTERS].rearrange("o (r c) -> o r c", c=FIRST_ROW_RUN),
            in_=first_row[0:1, :, 0:FIRST_ROW_RUN],
        )
